import numpy as np
import ml_dtypes


def mxq(x, axis, fmt="e4m3"):
    dtype, down = {"e4m3": (ml_dtypes.float8_e4m3fn, 7), "e5m2": (ml_dtypes.float8_e5m2, 14)}[fmt]
    v = np.moveaxis(np.asarray(x, np.float32).astype(ml_dtypes.bfloat16).astype(np.float64), axis, -1)
    blocks = v.reshape(v.shape[:-1] + (-1, 32))
    amax = np.abs(blocks).max(-1, keepdims=True)
    byte = np.maximum(np.where(amax > 0, np.frexp(amax)[1] - 1 + 127, 0) - down, 1)
    scale = np.exp2(byte - 127.0)
    codes = (blocks / scale).astype(np.float32).astype(dtype).astype(np.float64)
    return np.moveaxis((codes * scale).reshape(v.shape), -1, axis)


WIDE = False


def mx_kscale(k):
    if not WIDE:
        return np.ones(k)
    levels = np.array([10, -10, 5, -5, 0])
    a = np.random.permutation(np.resize(levels, k // 512 * 4)).reshape(k // 512, 4)
    idx = np.arange(k)
    return np.exp2(a[idx // 512, idx % 128 // 32])


BF16 = ml_dtypes.bfloat16


def bf(x):
    return np.asarray(x, np.float32).astype(BF16)


def f64(x):
    return np.asarray(x).astype(np.float64)


B, N, H = 4096, 512, 512


def get_mask(in_features, out_features, in_flow_features, mask_type=None):
    if mask_type == "input":
        in_degrees = np.arange(in_features) % in_flow_features
    else:
        in_degrees = np.arange(in_features) % (in_flow_features - 1)
    if mask_type == "output":
        out_degrees = np.arange(out_features) % in_flow_features - 1
    else:
        out_degrees = np.arange(out_features) % (in_flow_features - 1)
    return (out_degrees[:, None] >= in_degrees[None, :]) * 1.0


def setup_inputs():
    s, t = mx_kscale(H), mx_kscale(H)
    return {
        "inputs": bf(np.random.standard_normal((B, N))),
        "h_s1": bf(np.tanh(np.random.standard_normal((B, H))) * s),
        "h_t1": bf(np.maximum(np.random.standard_normal((B, H)), 0.0) * s),
        "s_w2": bf(np.random.standard_normal((H, H)) * 2.0 / np.sqrt(H) / s[None, :]),
        "s_b2": bf(np.random.standard_normal(H) * 0.2),
        "s_w3": bf(np.random.standard_normal((N, H)) * 2.0 / np.sqrt(H)),
        "s_b3": bf(np.random.standard_normal(N) * 0.2),
        "t_w2": bf(np.random.standard_normal((H, H)) * 2.0 / np.sqrt(H) / s[None, :] * t[:, None]),
        "t_b2": bf(np.random.standard_normal(H) * 0.2 * t),
        "t_w3": bf(np.random.standard_normal((N, H)) * 0.8 / np.sqrt(H) / t[None, :]),
        "t_b3": bf(np.random.standard_normal(N) * 0.1),
        "mask_hid": bf(get_mask(H, H, N)),
        "mask_out": bf(get_mask(H, N, N, "output")),
    }


def reference(inputs, h_s1, h_t1, s_w2, s_b2, s_w3, s_b3, t_w2, t_b2, t_w3, t_b3, mask_hid, mask_out):
    x = f64(inputs)
    mh = f64(mask_hid)
    mo = f64(mask_out)
    h = np.tanh((mxq(f64(h_s1), 1, "e4m3") @ mxq(f64(s_w2) * mh, 1, "e4m3").T) + f64(s_b2))
    m = (mxq(h, 1, "e4m3") @ mxq(f64(s_w3) * mo, 1, "e4m3").T) + f64(s_b3)
    h = np.maximum((mxq(f64(h_t1), 1, "e4m3") @ mxq(f64(t_w2) * mh, 1, "e4m3").T) + f64(t_b2), 0.0)
    a = (mxq(h, 1, "e4m3") @ mxq(f64(t_w3) * mo, 1, "e4m3").T) + f64(t_b3)
    u = (x - m) * np.exp(-a)
    logdet = -np.sum(a, axis=-1, keepdims=True)
    return (u, logdet)

@@ -1,0 +1,260 @@
+from contextlib import ExitStack
+
+import concourse.mybir as mybir
+from concourse.masks import make_identity
+
+F32 = mybir.dt.float32
+BF16 = mybir.dt.bfloat16
+U32 = mybir.dt.uint32
+U8 = mybir.dt.uint8
+FP8X4 = mybir.dt.float8_e4m3fn_x4
+ACT = mybir.ActivationFunctionType
+ALU = mybir.AluOpType
+
+P = 128
+B, N, H = 4096, 512, 512
+G = 8
+R = 4
+ROWS = B // P
+
+FLOPS = 4 * 2 * B * H * N
+
+H_ON_GPSIMD = True
+D_ENGINE = {"hs": "s", "ht": "v"}
+
+
+def tile_madesplit_pa_t_kernel(
+    tc, inputs, h_s1, h_t1, s_w2, s_b2, s_w3, s_b3, t_w2, t_b2, t_w3, t_b3, mask_hid, mask_out, out_0, out_1
+):
+    nc = tc.nc
+    with ExitStack() as ctx:
+        const = ctx.enter_context(tc.tile_pool(name="const", bufs=1))
+        wgrp_pool = ctx.enter_context(tc.tile_pool(name="wgrp", bufs=2))
+        raw_pool = ctx.enter_context(tc.tile_pool(name="raw", bufs=3))
+        mid_pool = ctx.enter_context(tc.tile_pool(name="mid", bufs=2))
+        epi_pool = ctx.enter_context(tc.tile_pool(name="epi", bufs=2))
+        ps_t = ctx.enter_context(tc.psum_pool(name="ps_t", bufs=2))
+        ps_1 = ctx.enter_context(tc.psum_pool(name="ps_1", bufs=3))
+        ps_2 = ctx.enter_context(tc.psum_pool(name="ps_2", bufs=3))
+
+        x_v = inputs.rearrange("(p i) n -> p i n", i=ROWS)
+        hs_v = h_s1.rearrange("(p i) k -> p i k", i=ROWS)
+        ht_v = h_t1.rearrange("(p i) k -> p i k", i=ROWS)
+        u_v = out_0.rearrange("(p i) n -> p i n", i=ROWS)
+
+        ident = const.tile([P, P], F32, name="ident")
+        make_identity(nc, ident[:])
+        ones = const.tile([P, P], BF16, name="ones")
+        nc.vector.memset(ones[:], 1.0)
+
+        raws = {}
+
+        views = {"hs": hs_v, "ht": ht_v, "x": x_v}
+
+        def load_one(nm, g):
+            t = raw_pool.tile([P, R * 512], BF16, name="raw_" + nm, tag="raw_" + nm)
+            nc.sync.dma_start(
+                out=t[:].rearrange("p (r k) -> p r k", r=R), in_=views[nm][:, R * g : R * g + R, :]
+            )
+            raws[(nm, g)] = t
+
+        def load(g):
+            for nm in ("hs", "ht", "x"):
+                load_one(nm, g)
+
+        def to_k_major(src, grouped, engines):
+            srcw = src[:].bitcast(F32)
+            dstw = grouped[:].bitcast(F32).rearrange("p (c u) -> p c u", u=2)
+            for half in range(2):
+                bank = ps_t.tile([P, 2, 256], F32, name="bank_t", tag="bank_t")
+                for rr in range(2):
+                    for u in range(2):
+                        o = 256 * (2 * half + rr) + 128 * u
+                        nc.tensor.transpose(bank[:, u, 128 * rr : 128 * rr + 128], srcw[:, o : o + 128], ident[:])
+                dst = dstw[:, 256 * half : 256 * half + 256, :]
+                src_p = bank[:].rearrange("p u c -> p c u")
+                if engines[half] == "v":
+                    nc.vector.tensor_copy(out=dst, in_=src_p)
+                else:
+                    nc.scalar.copy(out=dst, in_=src_p)
+
+        def quantise(grouped, nm, pool):
+            codes = pool.tile([P, 512], U32, name="codes_" + nm, tag="codes_" + nm, align_bytes=64)
+            scales = pool.tile([P, 512], U8, name="scales_" + nm, tag="scales_" + nm, align_bytes=64)
+            nc.vector.quantize_mx(out=codes[:].bitcast(FP8X4), scales=scales[:], in_=grouped[:])
+            return codes, scales
+
+        load_one("hs", 0)
+        w_raw = {}
+        hid_view = "(u p e) k -> p u e k"
+        out_view = "(r p) k -> p r k"
+
+        def load_w(nm, w, second_layer):
+            t = const.tile([P, 2048], BF16, name="w_" + nm)
+            if second_layer:
+                nc.sync.dma_start(
+                    out=t[:].rearrange("p (u e k) -> p u e k", u=2, e=2), in_=w.rearrange(hid_view, u=2, e=2)
+                )
+            else:
+                nc.sync.dma_start(out=t[:].rearrange("p (r k) -> p r k", r=4), in_=w.rearrange(out_view, p=P))
+            w_raw[nm] = t
+
+        load_w("s2", s_w2, True)
+        load_w("mh", mask_hid, True)
+        load_one("ht", 0)
+        load_w("t2", t_w2, True)
+
+        b2rows = const.tile([P, 256], BF16, name="b2rows")
+        nc.vector.memset(b2rows[:], 0.0)
+        nc.sync.dma_start(out=b2rows[0:2, :], in_=s_b2.rearrange("(u c) -> u c", u=2))
+        nc.sync.dma_start(out=b2rows[2:4, :], in_=t_b2.rearrange("(u c) -> u c", u=2))
+        b3rows = const.tile([P, 1024], BF16, name="b3rows")
+        nc.vector.memset(b3rows[:], 0.0)
+        nc.sync.dma_start(out=b3rows[0:1, 0:512], in_=s_b3.rearrange("(o c) -> o c", o=1))
+        nc.sync.dma_start(out=b3rows[0:1, 512:1024], in_=t_b3.rearrange("(o c) -> o c", o=1))
+
+        load_w("s3", s_w3, False)
+        load_w("mo", mask_out, False)
+        load_w("t3", t_w3, False)
+        load_one("x", 0)
+        load(1)
+
+        wq = {}
+
+        def prep_w(nm, mask, eng):
+            t = w_raw[nm]
+            eng.tensor_tensor(out=t[:], in0=t[:], in1=w_raw[mask][:], op=ALU.mult)
+            grouped = wgrp_pool.tile([P, 2048], BF16, name="wgrp", tag="wgrp", align_bytes=64)
+            to_k_major(t, grouped, ("s", "s"))
+            wq[nm] = quantise(grouped, "w" + nm, const)
+
+        h1q = {}
+
+        def stage0(g):
+            for nm in ("hs", "ht"):
+                grouped = mid_pool.tile([P, 2048], BF16, name="g1_" + nm, tag="g1_" + nm, align_bytes=64)
+                to_k_major(raws[(nm, g)], grouped, ("s", "s"))
+                h1q[(nm, g)] = quantise(grouped, "q1" + nm, mid_pool)
+
+        h2q = {}
+
+        def stage1(g):
+            for nm, wn, func, boff in (("hs", "s2", ACT.Tanh, 0), ("ht", "t2", ACT.Relu, 4)):
+                codes, scales = h1q[(nm, g)]
+                wc, ws = wq[wn]
+                h_t = mid_pool.tile([P, 4, 512], BF16, name="hT_" + nm, tag="hT_" + nm)
+                for j in range(4):
+                    acc = ps_1.tile([P, 512], F32, name="acc1", tag="acc1")
+                    nc.tensor.matmul_mx(
+                        out=acc[:],
+                        lhsT=wc[:, 128 * j : 128 * j + 128].bitcast(FP8X4),
+                        lhsT_scale=ws[:, 128 * j : 128 * j + 128],
+                        rhs=codes[:].bitcast(FP8X4),
+                        rhs_scale=scales[:],
+                        start=True,
+                        stop=True,
+                    )
+                    nc.scalar.activation(
+                        out=h_t[:, j, :], in_=acc[:], func=func, bias=b2f[:, boff + j : boff + j + 1], scale=1.0
+                    )
+                grouped = mid_pool.tile([P, 512, 4], BF16, name="g2_" + nm, tag="g2_" + nm, align_bytes=64)
+                if D_ENGINE[nm] == "v":
+                    nc.vector.tensor_copy(
+                        out=grouped[:].rearrange("p (c i) t -> p c t i", i=4),
+                        in_=h_t[:].rearrange("p t (c i) -> p c t i", i=4),
+                    )
+                else:
+                    nc.scalar.copy(
+                        out=grouped[:].rearrange("p (c i) t -> p c t i", i=4),
+                        in_=h_t[:].rearrange("p t (c i) -> p c t i", i=4),
+                    )
+                codes2 = mid_pool.tile([P, 512], U32, name="c2_" + nm, tag="c2_" + nm, align_bytes=64)
+                scales2 = mid_pool.tile([P, 512], U8, name="s2_" + nm, tag="s2_" + nm, align_bytes=64)
+                nc.vector.quantize_mx(
+                    out=codes2[:].bitcast(FP8X4), scales=scales2[:], in_=grouped[:].rearrange("p c t -> p (c t)")
+                )
+                h2q[(nm, g)] = (codes2, scales2)
+
+        xbs = {}
+
+        def shift_x(g):
+            xb = epi_pool.tile([P, R, 512], F32, name="xb", tag="xb")
+            eng = nc.gpsimd if H_ON_GPSIMD else nc.vector
+            eng.tensor_tensor(
+                out=xb[:],
+                in0=raws[("x", g)][:].rearrange("p (r n) -> p r n", r=R),
+                in1=nb3s[:].unsqueeze(1).to_broadcast([P, R, 512]),
+                op=ALU.add,
+            )
+            xbs[g] = xb
+
+        def stage2(g):
+            na = epi_pool.tile([P, R, 512], F32, name="na", tag="na")
+            d = epi_pool.tile([P, R, 512], F32, name="d", tag="d")
+            xb = xbs[g]
+            for r in range(R):
+                accs = {}
+                for nm, wn in (("ht", "t3"), ("hs", "s3")):
+                    codes, scales = h2q[(nm, g)]
+                    wc, ws = wq[wn]
+                    acc = ps_2.tile([P, 512], F32, name="acc2", tag="acc2")
+                    nc.tensor.matmul_mx(
+                        out=acc[:],
+                        lhsT=codes[:, 128 * r : 128 * r + 128].bitcast(FP8X4),
+                        lhsT_scale=scales[:, 128 * r : 128 * r + 128],
+                        rhs=wc[:].bitcast(FP8X4),
+                        rhs_scale=ws[:],
+                        start=True,
+                        stop=True,
+                    )
+                    accs[nm] = acc
+                col = R * g + r
+                nc.vector.scalar_tensor_tensor(
+                    out=na[:, r, :], in0=accs["ht"][:], scalar=-1.0, in1=nb3t[:], op0=ALU.mult, op1=ALU.add,
+                    accum_out=ld[:, col : col + 1],
+                )
+                nc.vector.scalar_tensor_tensor(
+                    out=d[:, r, :], in0=accs["hs"][:], scalar=-1.0, in1=xb[:, r, :], op0=ALU.mult, op1=ALU.add,
+                )
+                if g == G - 1:
+                    nc.scalar.activation(out=na[:, r, :], in_=na[:, r, :], func=ACT.Exp)
+                    nc.vector.tensor_tensor(out=d[:, r, :], in0=d[:, r, :], in1=na[:, r, :], op=ALU.mult)
+                    nc.sync.dma_start(out=u_v[:, R * g + r, :], in_=d[:, r, :])
+            if g < G - 1:
+                nc.scalar.activation(out=na[:], in_=na[:], func=ACT.Exp)
+                nc.vector.tensor_tensor(out=d[:], in0=d[:], in1=na[:], op=ALU.mult)
+                nc.sync.dma_start(out=u_v[:, R * g : R * g + R, :], in_=d[:])
+
+        stage0(0)
+        prep_w("s2", "mh", nc.vector)
+        prep_w("t2", "mh", nc.vector)
+
+        bank_b = ps_t.tile([P, P], F32, name="bank_b", tag="bank_t")
+        nc.tensor.transpose(bank_b[:], b2rows[:].bitcast(F32), ident[:])
+        b2w = const.tile([P, 4], F32, name="b2w")
+        nc.vector.tensor_copy(out=b2w[:], in_=bank_b[:, 0:4])
+        b2f = const.tile([P, 8], F32, name="b2f")
+        nc.vector.tensor_copy(out=b2f[:], in_=b2w[:].bitcast(BF16))
+
+        nb3s = const.tile([P, 512], F32, name="nb3s")
+        nb3t = const.tile([P, 512], F32, name="nb3t")
+        for dst, off in ((nb3s, 0), (nb3t, 512)):
+            bank_c = ps_1.tile([P, 512], F32, name="bank_c", tag="acc1")
+            nc.tensor.matmul(out=bank_c[:], lhsT=ones[:], rhs=b3rows[:, off : off + 512], start=True, stop=True)
+            nc.scalar.mul(out=dst[:], in_=bank_c[:], mul=-1.0)
+        ld = const.tile([P, ROWS], F32, name="ld")
+
+        prep_w("s3", "mo", nc.gpsimd)
+        prep_w("t3", "mo", nc.gpsimd)
+
+        for i in range(1, G + 2):
+            if i + 1 < G:
+                load(i + 1)
+            if i < G:
+                stage0(i)
+            if i - 1 < G:
+                shift_x(i - 1)
+                stage1(i - 1)
+            if i >= 2:
+                stage2(i - 2)
+        nc.sync.dma_start(out=out_1.rearrange("(p i) o -> p (i o)", i=ROWS), in_=ld[:])

@@ -19,7 +19,7 @@ ROWS = B // P
 
 FLOPS = 4 * 2 * B * H * N
 
-H_ON_GPSIMD = True
+H_ON_GPSIMD = False
 D_ENGINE = {"hs": "s", "ht": "v"}
 
 
@@ -244,8 +244,8 @@ def tile_madesplit_pa_t_kernel(
             nc.scalar.mul(out=dst[:], in_=bank_c[:], mul=-1.0)
         ld = const.tile([P, ROWS], F32, name="ld")
 
-        prep_w("s3", "mo", nc.gpsimd)
-        prep_w("t3", "mo", nc.gpsimd)
+        prep_w("s3", "mo", nc.vector)
+        prep_w("t3", "mo", nc.vector)
 
         for i in range(1, G + 2):
             if i + 1 < G:

@@ -19,7 +19,8 @@ ROWS = B // P
 
 FLOPS = 4 * 2 * B * H * N
 
-H_ON_GPSIMD = False
+H_ON_GPSIMD = True
+H_PIECE = 256
 D_ENGINE = {"hs": "s", "ht": "v"}
 
 
@@ -179,13 +180,15 @@ def tile_madesplit_pa_t_kernel(
 
         def shift_x(g):
             xb = epi_pool.tile([P, R, 512], F32, name="xb", tag="xb")
-            eng = nc.gpsimd if H_ON_GPSIMD else nc.vector
-            eng.tensor_tensor(
-                out=xb[:],
-                in0=raws[("x", g)][:].rearrange("p (r n) -> p r n", r=R),
-                in1=nb3s[:].unsqueeze(1).to_broadcast([P, R, 512]),
-                op=ALU.add,
-            )
+            xr = raws[("x", g)]
+            for r in range(R):
+                for c in range(0, 512, H_PIECE):
+                    nc.gpsimd.tensor_tensor(
+                        out=xb[:, r, c : c + H_PIECE],
+                        in0=xr[:, 512 * r + c : 512 * r + c + H_PIECE],
+                        in1=nb3s[:, c : c + H_PIECE],
+                        op=ALU.add,
+                    )
             xbs[g] = xb
 
         def stage2(g):

@@ -16,12 +16,15 @@ B, N, H = 4096, 512, 512
 G = 8
 R = 4
 ROWS = B // P
+ITEMS = G * R
 
 FLOPS = 4 * 2 * B * H * N
 
-H_ON_GPSIMD = True
+PINNED = True
 H_PIECE = 256
-D_ENGINE = {"hs": "s", "ht": "v"}
+OFF = {"B": 1, "Ct": 3, "Cs": 5, "Dt": 7, "Et": 8, "F": 8, "X": 9, "Ds": 9, "Es": 10, "I": 10, "J": 11, "H": 6}
+A_ON_V = 0
+CT_ON_V = 0
 
 
 def tile_madesplit_pa_t_kernel(
@@ -32,15 +35,16 @@ def tile_madesplit_pa_t_kernel(
         const = ctx.enter_context(tc.tile_pool(name="const", bufs=1))
         wgrp_pool = ctx.enter_context(tc.tile_pool(name="wgrp", bufs=2))
         raw_pool = ctx.enter_context(tc.tile_pool(name="raw", bufs=3))
-        mid_pool = ctx.enter_context(tc.tile_pool(name="mid", bufs=2))
-        epi_pool = ctx.enter_context(tc.tile_pool(name="epi", bufs=2))
-        ps_t = ctx.enter_context(tc.psum_pool(name="ps_t", bufs=2))
-        ps_1 = ctx.enter_context(tc.psum_pool(name="ps_1", bufs=3))
-        ps_2 = ctx.enter_context(tc.psum_pool(name="ps_2", bufs=3))
+        two = ctx.enter_context(tc.tile_pool(name="two", bufs=2))
+        three = ctx.enter_context(tc.tile_pool(name="three", bufs=3))
+        ps2 = ctx.enter_context(tc.psum_pool(name="ps2", bufs=2))
+        ps1 = ctx.enter_context(tc.psum_pool(name="ps1", bufs=1))
 
-        x_v = inputs.rearrange("(p i) n -> p i n", i=ROWS)
-        hs_v = h_s1.rearrange("(p i) k -> p i k", i=ROWS)
-        ht_v = h_t1.rearrange("(p i) k -> p i k", i=ROWS)
+        views = {
+            "x": inputs.rearrange("(p i) n -> p i n", i=ROWS),
+            "s": h_s1.rearrange("(p i) k -> p i k", i=ROWS),
+            "t": h_t1.rearrange("(p i) k -> p i k", i=ROWS),
+        }
         u_v = out_0.rearrange("(p i) n -> p i n", i=ROWS)
 
         ident = const.tile([P, P], F32, name="ident")
@@ -48,216 +52,297 @@ def tile_madesplit_pa_t_kernel(
         ones = const.tile([P, P], BF16, name="ones")
         nc.vector.memset(ones[:], 1.0)
 
-        raws = {}
+        st = {}
 
-        views = {"hs": hs_v, "ht": ht_v, "x": x_v}
+        def ok(n):
+            return 0 <= n < ITEMS
 
-        def load_one(nm, g):
-            t = raw_pool.tile([P, R * 512], BF16, name="raw_" + nm, tag="raw_" + nm)
-            nc.sync.dma_start(
-                out=t[:].rearrange("p (r k) -> p r k", r=R), in_=views[nm][:, R * g : R * g + R, :]
-            )
-            raws[(nm, g)] = t
-
-        def load(g):
-            for nm in ("hs", "ht", "x"):
-                load_one(nm, g)
-
-        def to_k_major(src, grouped, engines):
-            srcw = src[:].bitcast(F32)
-            dstw = grouped[:].bitcast(F32).rearrange("p (c u) -> p c u", u=2)
-            for half in range(2):
-                bank = ps_t.tile([P, 2, 256], F32, name="bank_t", tag="bank_t")
-                for rr in range(2):
-                    for u in range(2):
-                        o = 256 * (2 * half + rr) + 128 * u
-                        nc.tensor.transpose(bank[:, u, 128 * rr : 128 * rr + 128], srcw[:, o : o + 128], ident[:])
-                dst = dstw[:, 256 * half : 256 * half + 256, :]
-                src_p = bank[:].rearrange("p u c -> p c u")
-                if engines[half] == "v":
-                    nc.vector.tensor_copy(out=dst, in_=src_p)
-                else:
-                    nc.scalar.copy(out=dst, in_=src_p)
-
-        def quantise(grouped, nm, pool):
-            codes = pool.tile([P, 512], U32, name="codes_" + nm, tag="codes_" + nm, align_bytes=64)
-            scales = pool.tile([P, 512], U8, name="scales_" + nm, tag="scales_" + nm, align_bytes=64)
-            nc.vector.quantize_mx(out=codes[:].bitcast(FP8X4), scales=scales[:], in_=grouped[:])
-            return codes, scales
-
-        load_one("hs", 0)
-        w_raw = {}
-        hid_view = "(u p e) k -> p u e k"
-        out_view = "(r p) k -> p r k"
-
-        def load_w(nm, w, second_layer):
-            t = const.tile([P, 2048], BF16, name="w_" + nm)
-            if second_layer:
-                nc.sync.dma_start(
-                    out=t[:].rearrange("p (u e k) -> p u e k", u=2, e=2), in_=w.rearrange(hid_view, u=2, e=2)
-                )
+        def copy_on(eng, out, in_):
+            if eng == "v":
+                nc.vector.tensor_copy(out=out, in_=in_)
             else:
-                nc.sync.dma_start(out=t[:].rearrange("p (r k) -> p r k", r=4), in_=w.rearrange(out_view, p=P))
-            w_raw[nm] = t
+                nc.scalar.copy(out=out, in_=in_)
 
-        load_w("s2", s_w2, True)
-        load_w("mh", mask_hid, True)
-        load_one("ht", 0)
-        load_w("t2", t_w2, True)
+        def LD(nm, g):
+            if not 0 <= g < G:
+                return
+            t = raw_pool.tile([P, R * 512], BF16, name="raw_" + nm, tag="raw_" + nm, bufs=4 if nm == "x" else 3)
+            nc.sync.dma_start(out=t[:].rearrange("p (r k) -> p r k", r=R), in_=views[nm][:, R * g : R * g + R, :])
+            st[("raw", nm, g)] = t
 
+        w_dram = {"s2": s_w2, "t2": t_w2, "mh": mask_hid, "s3": s_w3, "t3": t_w3, "mo": mask_out}
+
+        def LDW(nm, h):
+            if h == 0:
+                st[("w", nm)] = const.tile([P, 2048], BF16, name="w_" + nm)
+            t = st[("w", nm)]
+            if nm in ("s2", "t2", "mh"):
+                src = w_dram[nm].rearrange("(u p e) k -> u p e k", u=2, e=2)[h]
+                nc.sync.dma_start(out=t[:, 1024 * h : 1024 * h + 1024].rearrange("p (e k) -> p e k", e=2), in_=src)
+            else:
+                src = w_dram[nm].rearrange("(r p) k -> p r k", p=P)[:, 2 * h : 2 * h + 2, :]
+                nc.sync.dma_start(out=t[:, 1024 * h : 1024 * h + 1024].rearrange("p (r k) -> p r k", r=2), in_=src)
+
+        def turn(src, h, tag, pool):
+            bank = pool.tile([P, 2, 256], F32, name="bank_" + tag, tag=tag)
+            srcw = src[:].bitcast(F32)
+            for rr in range(2):
+                for u in range(2):
+                    o = 256 * (2 * h + rr) + 128 * u
+                    nc.tensor.transpose(bank[:, u, 128 * rr : 128 * rr + 128], srcw[:, o : o + 128], ident[:])
+            return bank
+
+        def out_of_bank(bank, grouped, h, eng):
+            dstw = grouped[:].bitcast(F32).rearrange("p (c u) -> p c u", u=2)
+            copy_on(eng, dstw[:, 256 * h : 256 * h + 256, :], bank[:].rearrange("p u c -> p c u"))
+
+        def quantise(grouped2d, codes, scales, c0, c1):
+            nc.vector.quantize_mx(
+                out=codes[:, c0:c1].bitcast(FP8X4), scales=scales[:, c0:c1], in_=grouped2d[:, 4 * c0 : 4 * c1]
+            )
+
+        def prep_w(nm, mask, h, eng, tag, pool):
+            t = st[("w", nm)]
+            sl = slice(1024 * h, 1024 * h + 1024)
+            nc.vector.tensor_tensor(out=t[:, sl], in0=t[:, sl], in1=st[("w", mask)][:, sl], op=ALU.mult)
+            if h == 0:
+                st[("wg", nm)] = wgrp_pool.tile([P, 2048], BF16, name="wgrp", tag="wgrp", align_bytes=64)
+                st[("wc", nm)] = const.tile([P, 512], U32, name="wc_" + nm, align_bytes=64)
+                st[("ws", nm)] = const.tile([P, 512], U8, name="ws_" + nm, align_bytes=64)
+            bank = turn(t, h, tag, pool)
+            out_of_bank(bank, st[("wg", nm)], h, eng)
+            quantise(st[("wg", nm)], st[("wc", nm)], st[("ws", nm)], 256 * h, 256 * h + 256)
+
+        def T(n):
+            if not ok(n):
+                return
+            g, q = divmod(n, 4)
+            nm = "t" if q < 2 else "s"
+            st[("b0", n)] = turn(st[("raw", nm, g)], q % 2, "tp", ps2)
+
+        def A(n, eng):
+            if not ok(n):
+                return
+            g, q = divmod(n, 4)
+            nm = "t" if q < 2 else "s"
+            if q % 2 == 0:
+                st[("g1", nm, g)] = two.tile([P, 2048], BF16, name="g1_" + nm, tag="g1_" + nm, align_bytes=64)
+            out_of_bank(st[("b0", n)], st[("g1", nm, g)], q % 2, eng)
+
+        def Bq(n):
+            if not ok(n):
+                return
+            g, q = divmod(n, 4)
+            nm = "t" if q < 2 else "s"
+            h = q % 2
+            if h == 0:
+                st[("c1", nm, g)] = three.tile([P, 512], U32, name="c1_" + nm, tag="c1_" + nm, align_bytes=64)
+                st[("s1", nm, g)] = three.tile([P, 512], U8, name="s1_" + nm, tag="s1_" + nm, align_bytes=64)
+            quantise(st[("g1", nm, g)], st[("c1", nm, g)], st[("s1", nm, g)], 256 * h, 256 * h + 256)
+
+        def M1(nm, n):
+            if not ok(n):
+                return
+            g, j = divmod(n, 4)
+            acc = ps2.tile([P, 512], F32, name="m1" + nm, tag="m1" + nm)
+            nc.tensor.matmul_mx(
+                out=acc[:],
+                lhsT=st[("wc", nm + "2")][:, 128 * j : 128 * j + 128].bitcast(FP8X4),
+                lhsT_scale=st[("ws", nm + "2")][:, 128 * j : 128 * j + 128],
+                rhs=st[("c1", nm, g)][:].bitcast(FP8X4),
+                rhs_scale=st[("s1", nm, g)][:],
+                start=True,
+                stop=True,
+            )
+            st[("a1", nm, n)] = acc
+
+        def C(nm, n, eng):
+            if not ok(n):
+                return
+            g, j = divmod(n, 4)
+            if j == 0:
+                st[("hT", nm, g)] = two.tile([P, 4, 512], BF16, name="hT_" + nm, tag="hT_" + nm)
+            dst = st[("hT", nm, g)][:, j, :]
+            acc = st[("a1", nm, n)]
+            boff = 0 if nm == "s" else 4
+            bias = b2f[:, boff + j : boff + j + 1]
+            if eng == "v":
+                nc.vector.tensor_scalar(out=dst, in0=acc[:], scalar1=bias, scalar2=0.0, op0=ALU.add, op1=ALU.max)
+            else:
+                nc.scalar.activation(out=dst, in_=acc[:], func=ACT.Tanh if nm == "s" else ACT.Relu, bias=bias, scale=1.0)
+
+        def D(nm, n, eng):
+            if not ok(n):
+                return
+            g, q = divmod(n, 4)
+            if q == 0:
+                st[("g2", nm, g)] = two.tile([P, 512, 4], BF16, name="g2_" + nm, tag="g2_" + nm, align_bytes=64)
+            c = slice(128 * q, 128 * q + 128)
+            copy_on(
+                eng,
+                st[("g2", nm, g)][:, c, :].rearrange("p (c i) t -> p c t i", i=4),
+                st[("hT", nm, g)][:, :, c].rearrange("p t (c i) -> p c t i", i=4),
+            )
+
+        def E(nm, n):
+            if not ok(n):
+                return
+            g, q = divmod(n, 4)
+            if q == 0:
+                st[("c2", nm, g)] = two.tile([P, 512], U32, name="c2_" + nm, tag="c2_" + nm, align_bytes=64)
+                st[("s2", nm, g)] = two.tile([P, 512], U8, name="s2_" + nm, tag="s2_" + nm, align_bytes=64)
+            quantise(
+                st[("g2", nm, g)][:].rearrange("p c t -> p (c t)"), st[("c2", nm, g)], st[("s2", nm, g)],
+                128 * q, 128 * q + 128,
+            )
+
+        def M2(nm, n):
+            if not ok(n):
+                return
+            g, q = divmod(n, 4)
+            acc = ps1.tile([P, 512], F32, name="m2" + nm, tag="m2" + nm)
+            nc.tensor.matmul_mx(
+                out=acc[:],
+                lhsT=st[("c2", nm, g)][:, 128 * q : 128 * q + 128].bitcast(FP8X4),
+                lhsT_scale=st[("s2", nm, g)][:, 128 * q : 128 * q + 128],
+                rhs=st[("wc", nm + "3")][:].bitcast(FP8X4),
+                rhs_scale=st[("ws", nm + "3")][:],
+                start=True,
+                stop=True,
+            )
+            st[("a2", nm, n)] = acc
+
+        def Hx(n):
+            if not ok(n):
+                return
+            g, q = divmod(n, 4)
+            if q == 0:
+                st[("xb", g)] = two.tile([P, R, 512], F32, name="xb", tag="xb")
+            xr = st[("raw", "x", g)]
+            for c in range(0, 512, H_PIECE):
+                nc.gpsimd.tensor_tensor(
+                    out=st[("xb", g)][:, q, c : c + H_PIECE],
+                    in0=xr[:, 512 * q + c : 512 * q + c + H_PIECE],
+                    in1=nb3s[:, c : c + H_PIECE],
+                    op=ALU.add,
+                )
+
+        def Fa(n):
+            if not ok(n):
+                return
+            g, q = divmod(n, 4)
+            if q == 0:
+                st[("na", g)] = two.tile([P, R, 512], F32, name="na", tag="na")
+            nc.vector.scalar_tensor_tensor(
+                out=st[("na", g)][:, q, :], in0=st[("a2", "t", n)][:], scalar=-1.0, in1=nb3t[:],
+                op0=ALU.mult, op1=ALU.add, accum_out=ld[:, n : n + 1],
+            )
+
+        def Im(n):
+            if not ok(n):
+                return
+            g, q = divmod(n, 4)
+            if q == 0:
+                st[("d", g)] = three.tile([P, R, 512], F32, name="d", tag="d")
+            nc.vector.scalar_tensor_tensor(
+                out=st[("d", g)][:, q, :], in0=st[("a2", "s", n)][:], scalar=-1.0, in1=st[("xb", g)][:, q, :],
+                op0=ALU.mult, op1=ALU.add,
+            )
+
+        def X(n):
+            if not ok(n):
+                return
+            g, q = divmod(n, 4)
+            nc.scalar.activation(out=st[("na", g)][:, q, :], in_=st[("na", g)][:, q, :], func=ACT.Exp)
+
+        def J(n):
+            if not ok(n):
+                return
+            g, q = divmod(n, 4)
+            d = st[("d", g)]
+            nc.vector.tensor_tensor(out=d[:, q, :], in0=d[:, q, :], in1=st[("na", g)][:, q, :], op=ALU.mult)
+            if g == G - 1:
+                nc.sync.dma_start(out=u_v[:, n, :], in_=d[:, q, :])
+            elif q == R - 1:
+                nc.sync.dma_start(out=u_v[:, R * g : R * g + R, :], in_=d[:])
+
+        LDW("t2", 0)
+        LDW("mh", 0)
+        LD("t", 0)
+        LDW("t2", 1)
+        LDW("mh", 1)
         b2rows = const.tile([P, 256], BF16, name="b2rows")
         nc.vector.memset(b2rows[:], 0.0)
         nc.sync.dma_start(out=b2rows[0:2, :], in_=s_b2.rearrange("(u c) -> u c", u=2))
         nc.sync.dma_start(out=b2rows[2:4, :], in_=t_b2.rearrange("(u c) -> u c", u=2))
+        LD("s", 0)
+        LDW("s2", 0)
+        LDW("s2", 1)
+        LD("t", 1)
+        LD("s", 1)
         b3rows = const.tile([P, 1024], BF16, name="b3rows")
         nc.vector.memset(b3rows[:], 0.0)
         nc.sync.dma_start(out=b3rows[0:1, 0:512], in_=s_b3.rearrange("(o c) -> o c", o=1))
         nc.sync.dma_start(out=b3rows[0:1, 512:1024], in_=t_b3.rearrange("(o c) -> o c", o=1))
+        for nm in ("t3", "mo", "s3"):
+            LDW(nm, 0)
+            LDW(nm, 1)
+        LD("x", 0)
+        LD("t", 2)
+        LD("s", 2)
+        LD("x", 1)
 
-        load_w("s3", s_w3, False)
-        load_w("mo", mask_out, False)
-        load_w("t3", t_w3, False)
-        load_one("x", 0)
-        load(1)
+        prep_w("t2", "mh", 0, "s", "m2t", ps1)
+        prep_w("t2", "mh", 1, "s", "m2s", ps1)
 
-        wq = {}
-
-        def prep_w(nm, mask, eng):
-            t = w_raw[nm]
-            eng.tensor_tensor(out=t[:], in0=t[:], in1=w_raw[mask][:], op=ALU.mult)
-            grouped = wgrp_pool.tile([P, 2048], BF16, name="wgrp", tag="wgrp", align_bytes=64)
-            to_k_major(t, grouped, ("s", "s"))
-            wq[nm] = quantise(grouped, "w" + nm, const)
-
-        h1q = {}
-
-        def stage0(g):
-            for nm in ("hs", "ht"):
-                grouped = mid_pool.tile([P, 2048], BF16, name="g1_" + nm, tag="g1_" + nm, align_bytes=64)
-                to_k_major(raws[(nm, g)], grouped, ("s", "s"))
-                h1q[(nm, g)] = quantise(grouped, "q1" + nm, mid_pool)
-
-        h2q = {}
-
-        def stage1(g):
-            for nm, wn, func, boff in (("hs", "s2", ACT.Tanh, 0), ("ht", "t2", ACT.Relu, 4)):
-                codes, scales = h1q[(nm, g)]
-                wc, ws = wq[wn]
-                h_t = mid_pool.tile([P, 4, 512], BF16, name="hT_" + nm, tag="hT_" + nm)
-                for j in range(4):
-                    acc = ps_1.tile([P, 512], F32, name="acc1", tag="acc1")
-                    nc.tensor.matmul_mx(
-                        out=acc[:],
-                        lhsT=wc[:, 128 * j : 128 * j + 128].bitcast(FP8X4),
-                        lhsT_scale=ws[:, 128 * j : 128 * j + 128],
-                        rhs=codes[:].bitcast(FP8X4),
-                        rhs_scale=scales[:],
-                        start=True,
-                        stop=True,
-                    )
-                    nc.scalar.activation(
-                        out=h_t[:, j, :], in_=acc[:], func=func, bias=b2f[:, boff + j : boff + j + 1], scale=1.0
-                    )
-                grouped = mid_pool.tile([P, 512, 4], BF16, name="g2_" + nm, tag="g2_" + nm, align_bytes=64)
-                if D_ENGINE[nm] == "v":
-                    nc.vector.tensor_copy(
-                        out=grouped[:].rearrange("p (c i) t -> p c t i", i=4),
-                        in_=h_t[:].rearrange("p t (c i) -> p c t i", i=4),
-                    )
-                else:
-                    nc.scalar.copy(
-                        out=grouped[:].rearrange("p (c i) t -> p c t i", i=4),
-                        in_=h_t[:].rearrange("p t (c i) -> p c t i", i=4),
-                    )
-                codes2 = mid_pool.tile([P, 512], U32, name="c2_" + nm, tag="c2_" + nm, align_bytes=64)
-                scales2 = mid_pool.tile([P, 512], U8, name="s2_" + nm, tag="s2_" + nm, align_bytes=64)
-                nc.vector.quantize_mx(
-                    out=codes2[:].bitcast(FP8X4), scales=scales2[:], in_=grouped[:].rearrange("p c t -> p (c t)")
-                )
-                h2q[(nm, g)] = (codes2, scales2)
-
-        xbs = {}
-
-        def shift_x(g):
-            xb = epi_pool.tile([P, R, 512], F32, name="xb", tag="xb")
-            xr = raws[("x", g)]
-            for r in range(R):
-                for c in range(0, 512, H_PIECE):
-                    nc.gpsimd.tensor_tensor(
-                        out=xb[:, r, c : c + H_PIECE],
-                        in0=xr[:, 512 * r + c : 512 * r + c + H_PIECE],
-                        in1=nb3s[:, c : c + H_PIECE],
-                        op=ALU.add,
-                    )
-            xbs[g] = xb
-
-        def stage2(g):
-            na = epi_pool.tile([P, R, 512], F32, name="na", tag="na")
-            d = epi_pool.tile([P, R, 512], F32, name="d", tag="d")
-            xb = xbs[g]
-            for r in range(R):
-                accs = {}
-                for nm, wn in (("ht", "t3"), ("hs", "s3")):
-                    codes, scales = h2q[(nm, g)]
-                    wc, ws = wq[wn]
-                    acc = ps_2.tile([P, 512], F32, name="acc2", tag="acc2")
-                    nc.tensor.matmul_mx(
-                        out=acc[:],
-                        lhsT=codes[:, 128 * r : 128 * r + 128].bitcast(FP8X4),
-                        lhsT_scale=scales[:, 128 * r : 128 * r + 128],
-                        rhs=wc[:].bitcast(FP8X4),
-                        rhs_scale=ws[:],
-                        start=True,
-                        stop=True,
-                    )
-                    accs[nm] = acc
-                col = R * g + r
-                nc.vector.scalar_tensor_tensor(
-                    out=na[:, r, :], in0=accs["ht"][:], scalar=-1.0, in1=nb3t[:], op0=ALU.mult, op1=ALU.add,
-                    accum_out=ld[:, col : col + 1],
-                )
-                nc.vector.scalar_tensor_tensor(
-                    out=d[:, r, :], in0=accs["hs"][:], scalar=-1.0, in1=xb[:, r, :], op0=ALU.mult, op1=ALU.add,
-                )
-                if g == G - 1:
-                    nc.scalar.activation(out=na[:, r, :], in_=na[:, r, :], func=ACT.Exp)
-                    nc.vector.tensor_tensor(out=d[:, r, :], in0=d[:, r, :], in1=na[:, r, :], op=ALU.mult)
-                    nc.sync.dma_start(out=u_v[:, R * g + r, :], in_=d[:, r, :])
-            if g < G - 1:
-                nc.scalar.activation(out=na[:], in_=na[:], func=ACT.Exp)
-                nc.vector.tensor_tensor(out=d[:], in0=d[:], in1=na[:], op=ALU.mult)
-                nc.sync.dma_start(out=u_v[:, R * g : R * g + R, :], in_=d[:])
-
-        stage0(0)
-        prep_w("s2", "mh", nc.vector)
-        prep_w("t2", "mh", nc.vector)
-
-        bank_b = ps_t.tile([P, P], F32, name="bank_b", tag="bank_t")
+        bank_b = ps1.tile([P, P], F32, name="bank_b", tag="m2t")
         nc.tensor.transpose(bank_b[:], b2rows[:].bitcast(F32), ident[:])
         b2w = const.tile([P, 4], F32, name="b2w")
         nc.vector.tensor_copy(out=b2w[:], in_=bank_b[:, 0:4])
         b2f = const.tile([P, 8], F32, name="b2f")
         nc.vector.tensor_copy(out=b2f[:], in_=b2w[:].bitcast(BF16))
 
+        prep_w("s2", "mh", 0, "v", "m2t", ps1)
+        prep_w("s2", "mh", 1, "v", "m2s", ps1)
+
         nb3s = const.tile([P, 512], F32, name="nb3s")
         nb3t = const.tile([P, 512], F32, name="nb3t")
-        for dst, off in ((nb3s, 0), (nb3t, 512)):
-            bank_c = ps_1.tile([P, 512], F32, name="bank_c", tag="acc1")
+        for dst, off, tag in ((nb3s, 0, "m2t"), (nb3t, 512, "m2s")):
+            bank_c = ps1.tile([P, 512], F32, name="bank_c", tag=tag)
             nc.tensor.matmul(out=bank_c[:], lhsT=ones[:], rhs=b3rows[:, off : off + 512], start=True, stop=True)
-            nc.scalar.mul(out=dst[:], in_=bank_c[:], mul=-1.0)
+            nc.vector.tensor_scalar(out=dst[:], in0=bank_c[:], scalar1=-1.0, scalar2=0.0, op0=ALU.mult, op1=ALU.add)
         ld = const.tile([P, ROWS], F32, name="ld")
 
-        prep_w("s3", "mo", nc.vector)
-        prep_w("t3", "mo", nc.vector)
+        prep_w("t3", "mo", 0, "v", "m2t", ps1)
+        prep_w("t3", "mo", 1, "v", "m2s", ps1)
+        prep_w("s3", "mo", 0, "v", "m2t", ps1)
+        prep_w("s3", "mo", 1, "v", "m2s", ps1)
 
-        for i in range(1, G + 2):
-            if i + 1 < G:
-                load(i + 1)
-            if i < G:
-                stage0(i)
-            if i - 1 < G:
-                shift_x(i - 1)
-                stage1(i - 1)
-            if i >= 2:
-                stage2(i - 2)
+        if PINNED:
+            ctx.enter_context(tc.manual_schedule())
+
+        T(0)
+        for s in range(ITEMS + OFF["J"]):
+            Bq(s - OFF["B"])
+            E("t", s - OFF["Et"])
+            E("s", s - OFF["Es"])
+            M2("t", s - OFF["F"])
+            M2("s", s - OFF["I"])
+            C("t", s - OFF["Ct"], "v" if s - OFF["Ct"] < CT_ON_V else "s")
+            C("s", s - OFF["Cs"], "s")
+            A(s, "v" if s < A_ON_V else "s")
+            D("t", s - OFF["Dt"], "v")
+            D("s", s - OFF["Ds"], "s")
+            X(s - OFF["X"])
+            J(s - OFF["J"])
+            Fa(s - OFF["F"])
+            Im(s - OFF["I"])
+            M1("t", s + 1 - OFF["Ct"])
+            M1("s", s + 1 - OFF["Cs"])
+            T(s + 1)
+            Hx(s - OFF["H"])
+            if s % 4 == 0:
+                LD("t", s // 4 + 3)
+                LD("s", s // 4 + 3)
+                LD("x", s // 4 + 2)
         nc.sync.dma_start(out=out_1.rearrange("(p i) o -> p (i o)", i=ROWS), in_=ld[:])

@@ -24,7 +24,10 @@ PINNED = True
 H_PIECE = 256
 OFF = {"B": 1, "Ct": 3, "Cs": 5, "Dt": 7, "Et": 8, "F": 8, "X": 9, "Ds": 9, "Es": 10, "I": 10, "J": 11, "H": 6}
 A_ON_V = 0
-CT_ON_V = 0
+CT_ON_V = 8
+DT_ON_S_FROM = 28
+MASK_ON_G = ()
+J_ON_G = (27, 28, 29, 30)
 
 
 def tile_madesplit_pa_t_kernel(
@@ -104,7 +107,14 @@ def tile_madesplit_pa_t_kernel(
         def prep_w(nm, mask, h, eng, tag, pool):
             t = st[("w", nm)]
             sl = slice(1024 * h, 1024 * h + 1024)
-            nc.vector.tensor_tensor(out=t[:, sl], in0=t[:, sl], in1=st[("w", mask)][:, sl], op=ALU.mult)
+            if nm in MASK_ON_G:
+                for c in range(1024 * h, 1024 * h + 1024, H_PIECE):
+                    nc.gpsimd.tensor_tensor(
+                        out=t[:, c : c + H_PIECE], in0=t[:, c : c + H_PIECE], in1=st[("w", mask)][:, c : c + H_PIECE],
+                        op=ALU.mult,
+                    )
+            else:
+                nc.vector.tensor_tensor(out=t[:, sl], in0=t[:, sl], in1=st[("w", mask)][:, sl], op=ALU.mult)
             if h == 0:
                 st[("wg", nm)] = wgrp_pool.tile([P, 2048], BF16, name="wgrp", tag="wgrp", align_bytes=64)
                 st[("wc", nm)] = const.tile([P, 512], U32, name="wc_" + nm, align_bytes=64)
@@ -260,7 +270,14 @@ def tile_madesplit_pa_t_kernel(
                 return
             g, q = divmod(n, 4)
             d = st[("d", g)]
-            nc.vector.tensor_tensor(out=d[:, q, :], in0=d[:, q, :], in1=st[("na", g)][:, q, :], op=ALU.mult)
+            if n in J_ON_G:
+                for c in range(0, 512, H_PIECE):
+                    nc.gpsimd.tensor_tensor(
+                        out=d[:, q, c : c + H_PIECE], in0=d[:, q, c : c + H_PIECE],
+                        in1=st[("na", g)][:, q, c : c + H_PIECE], op=ALU.mult,
+                    )
+            else:
+                nc.vector.tensor_tensor(out=d[:, q, :], in0=d[:, q, :], in1=st[("na", g)][:, q, :], op=ALU.mult)
             if g == G - 1:
                 nc.sync.dma_start(out=u_v[:, n, :], in_=d[:, q, :])
             elif q == R - 1:
@@ -302,21 +319,21 @@ def tile_madesplit_pa_t_kernel(
         b2f = const.tile([P, 8], F32, name="b2f")
         nc.vector.tensor_copy(out=b2f[:], in_=b2w[:].bitcast(BF16))
 
-        prep_w("s2", "mh", 0, "v", "m2t", ps1)
-        prep_w("s2", "mh", 1, "v", "m2s", ps1)
+        prep_w("s2", "mh", 0, "s", "m2t", ps1)
+        prep_w("s2", "mh", 1, "s", "m2s", ps1)
 
         nb3s = const.tile([P, 512], F32, name="nb3s")
         nb3t = const.tile([P, 512], F32, name="nb3t")
         for dst, off, tag in ((nb3s, 0, "m2t"), (nb3t, 512, "m2s")):
             bank_c = ps1.tile([P, 512], F32, name="bank_c", tag=tag)
             nc.tensor.matmul(out=bank_c[:], lhsT=ones[:], rhs=b3rows[:, off : off + 512], start=True, stop=True)
-            nc.vector.tensor_scalar(out=dst[:], in0=bank_c[:], scalar1=-1.0, scalar2=0.0, op0=ALU.mult, op1=ALU.add)
+            nc.scalar.mul(out=dst[:], in_=bank_c[:], mul=-1.0)
         ld = const.tile([P, ROWS], F32, name="ld")
 
-        prep_w("t3", "mo", 0, "v", "m2t", ps1)
-        prep_w("t3", "mo", 1, "v", "m2s", ps1)
-        prep_w("s3", "mo", 0, "v", "m2t", ps1)
-        prep_w("s3", "mo", 1, "v", "m2s", ps1)
+        prep_w("t3", "mo", 0, "s", "m2t", ps1)
+        prep_w("t3", "mo", 1, "s", "m2s", ps1)
+        prep_w("s3", "mo", 0, "s", "m2t", ps1)
+        prep_w("s3", "mo", 1, "s", "m2s", ps1)
 
         if PINNED:
             ctx.enter_context(tc.manual_schedule())
@@ -331,7 +348,7 @@ def tile_madesplit_pa_t_kernel(
             C("t", s - OFF["Ct"], "v" if s - OFF["Ct"] < CT_ON_V else "s")
             C("s", s - OFF["Cs"], "s")
             A(s, "v" if s < A_ON_V else "s")
-            D("t", s - OFF["Dt"], "v")
+            D("t", s - OFF["Dt"], "s" if s - OFF["Dt"] >= DT_ON_S_FROM else "v")
             D("s", s - OFF["Ds"], "s")
             X(s - OFF["X"])
             J(s - OFF["J"])

@@ -21,7 +21,7 @@ ITEMS = G * R
 FLOPS = 4 * 2 * B * H * N
 
 PINNED = True
-H_PIECE = 256
+H_PIECE = 512
 OFF = {"B": 1, "Ct": 3, "Cs": 5, "Dt": 7, "Et": 8, "F": 8, "X": 9, "Ds": 9, "Es": 10, "I": 10, "J": 11, "H": 6}
 A_ON_V = 0
 CT_ON_V = 8

@@ -21,8 +21,8 @@ ITEMS = G * R
 FLOPS = 4 * 2 * B * H * N
 
 PINNED = True
-H_PIECE = 512
-OFF = {"B": 1, "Ct": 3, "Cs": 5, "Dt": 7, "Et": 8, "F": 8, "X": 9, "Ds": 9, "Es": 10, "I": 10, "J": 11, "H": 6}
+H_PIECE = 256
+OFF = {"B": 1, "Ct": 3, "Cs": 5, "Dt": 7, "Et": 8, "F": 9, "X": 10, "Ds": 9, "Es": 10, "I": 11, "J": 12, "H": 6}
 A_ON_V = 0
 CT_ON_V = 8
 DT_ON_S_FROM = 28
@@ -340,23 +340,23 @@ def tile_madesplit_pa_t_kernel(
 
         T(0)
         for s in range(ITEMS + OFF["J"]):
-            Bq(s - OFF["B"])
             E("t", s - OFF["Et"])
-            E("s", s - OFF["Es"])
-            M2("t", s - OFF["F"])
+            Bq(s - OFF["B"])
             M2("s", s - OFF["I"])
             C("t", s - OFF["Ct"], "v" if s - OFF["Ct"] < CT_ON_V else "s")
             C("s", s - OFF["Cs"], "s")
             A(s, "v" if s < A_ON_V else "s")
+            M1("t", s + 1 - OFF["Ct"])
+            T(s + 1)
+            M1("s", s + 1 - OFF["Cs"])
             D("t", s - OFF["Dt"], "s" if s - OFF["Dt"] >= DT_ON_S_FROM else "v")
             D("s", s - OFF["Ds"], "s")
             X(s - OFF["X"])
             J(s - OFF["J"])
+            E("s", s - OFF["Es"])
             Fa(s - OFF["F"])
+            M2("t", s + 1 - OFF["F"])
             Im(s - OFF["I"])
-            M1("t", s + 1 - OFF["Ct"])
-            M1("s", s + 1 - OFF["Cs"])
-            T(s + 1)
             Hx(s - OFF["H"])
             if s % 4 == 0:
                 LD("t", s // 4 + 3)

@@ -24,10 +24,10 @@ PINNED = True
 H_PIECE = 256
 OFF = {"B": 1, "Ct": 3, "Cs": 5, "Dt": 7, "Et": 8, "F": 9, "X": 10, "Ds": 9, "Es": 10, "I": 11, "J": 12, "H": 6}
 A_ON_V = 0
-CT_ON_V = 8
-DT_ON_S_FROM = 28
+CT_ON_V = 6
+DT_ON_S_FROM = 24
 MASK_ON_G = ()
-J_ON_G = (27, 28, 29, 30)
+J_ON_G = (26, 27, 28, 29, 30)
 
 
 def tile_madesplit_pa_t_kernel(

@@ -22,7 +22,8 @@ FLOPS = 4 * 2 * B * H * N
 
 PINNED = True
 H_PIECE = 256
-OFF = {"B": 1, "Ct": 3, "Cs": 5, "Dt": 7, "Et": 8, "F": 9, "X": 10, "Ds": 9, "Es": 10, "I": 11, "J": 12, "H": 6}
+XB_BUFS = 6
+OFF = {"B": 1, "Ct": 3, "Cs": 5, "Dt": 5, "Et": 6, "F": 7, "X": 8, "Ds": 6, "Es": 7, "I": 8, "J": 9, "H": 3}
 A_ON_V = 0
 CT_ON_V = 6
 DT_ON_S_FROM = 24
@@ -154,7 +155,7 @@ def tile_madesplit_pa_t_kernel(
             if not ok(n):
                 return
             g, j = divmod(n, 4)
-            acc = ps2.tile([P, 512], F32, name="m1" + nm, tag="m1" + nm)
+            acc = ps2.tile([P, 512], F32, name="m1", tag="m1", bufs=4)
             nc.tensor.matmul_mx(
                 out=acc[:],
                 lhsT=st[("wc", nm + "2")][:, 128 * j : 128 * j + 128].bitcast(FP8X4),
@@ -226,23 +227,18 @@ def tile_madesplit_pa_t_kernel(
             if not ok(n):
                 return
             g, q = divmod(n, 4)
-            if q == 0:
-                st[("xb", g)] = two.tile([P, R, 512], F32, name="xb", tag="xb")
+            st[("xb", n)] = two.tile([P, 512], F32, name="xb", tag="xb", bufs=XB_BUFS)
             xr = st[("raw", "x", g)]
-            for c in range(0, 512, H_PIECE):
-                nc.gpsimd.tensor_tensor(
-                    out=st[("xb", g)][:, q, c : c + H_PIECE],
-                    in0=xr[:, 512 * q + c : 512 * q + c + H_PIECE],
-                    in1=nb3s[:, c : c + H_PIECE],
-                    op=ALU.add,
-                )
+            nc.gpsimd.tensor_tensor(
+                out=st[("xb", n)][:], in0=xr[:, 512 * q : 512 * q + 512], in1=nb3s[:], op=ALU.add
+            )
 
         def Fa(n):
             if not ok(n):
                 return
             g, q = divmod(n, 4)
             if q == 0:
-                st[("na", g)] = two.tile([P, R, 512], F32, name="na", tag="na")
+                st[("na", g)] = three.tile([P, R, 512], F32, name="na", tag="na")
             nc.vector.scalar_tensor_tensor(
                 out=st[("na", g)][:, q, :], in0=st[("a2", "t", n)][:], scalar=-1.0, in1=nb3t[:],
                 op0=ALU.mult, op1=ALU.add, accum_out=ld[:, n : n + 1],
@@ -251,11 +247,8 @@ def tile_madesplit_pa_t_kernel(
         def Im(n):
             if not ok(n):
                 return
-            g, q = divmod(n, 4)
-            if q == 0:
-                st[("d", g)] = three.tile([P, R, 512], F32, name="d", tag="d")
             nc.vector.scalar_tensor_tensor(
-                out=st[("d", g)][:, q, :], in0=st[("a2", "s", n)][:], scalar=-1.0, in1=st[("xb", g)][:, q, :],
+                out=st[("xb", n)][:], in0=st[("a2", "s", n)][:], scalar=-1.0, in1=st[("xb", n)][:],
                 op0=ALU.mult, op1=ALU.add,
             )
 
@@ -269,19 +262,20 @@ def tile_madesplit_pa_t_kernel(
             if not ok(n):
                 return
             g, q = divmod(n, 4)
-            d = st[("d", g)]
+            d = st[("xb", n)]
+            u = st[("na", g)]
             if n in J_ON_G:
                 for c in range(0, 512, H_PIECE):
                     nc.gpsimd.tensor_tensor(
-                        out=d[:, q, c : c + H_PIECE], in0=d[:, q, c : c + H_PIECE],
-                        in1=st[("na", g)][:, q, c : c + H_PIECE], op=ALU.mult,
+                        out=u[:, q, c : c + H_PIECE], in0=d[:, c : c + H_PIECE],
+                        in1=u[:, q, c : c + H_PIECE], op=ALU.mult,
                     )
             else:
-                nc.vector.tensor_tensor(out=d[:, q, :], in0=d[:, q, :], in1=st[("na", g)][:, q, :], op=ALU.mult)
+                nc.vector.tensor_tensor(out=u[:, q, :], in0=d[:], in1=u[:, q, :], op=ALU.mult)
             if g == G - 1:
-                nc.sync.dma_start(out=u_v[:, n, :], in_=d[:, q, :])
+                nc.sync.dma_start(out=u_v[:, n, :], in_=u[:, q, :])
             elif q == R - 1:
-                nc.sync.dma_start(out=u_v[:, R * g : R * g + R, :], in_=d[:])
+                nc.sync.dma_start(out=u_v[:, R * g : R * g + R, :], in_=u[:])
 
         LDW("t2", 0)
         LDW("mh", 0)
@@ -307,7 +301,6 @@ def tile_madesplit_pa_t_kernel(
         LD("x", 0)
         LD("t", 2)
         LD("s", 2)
-        LD("x", 1)
 
         prep_w("t2", "mh", 0, "s", "m2t", ps1)
         prep_w("t2", "mh", 1, "s", "m2s", ps1)
@@ -338,17 +331,28 @@ def tile_madesplit_pa_t_kernel(
         if PINNED:
             ctx.enter_context(tc.manual_schedule())
 
+        def chunks(s, off):
+            g, r = divmod(s - off, 4)
+            return (4 * g + 2 * r, 4 * g + 2 * r + 1) if r < 2 else ()
+
         T(0)
+        T(1)
         for s in range(ITEMS + OFF["J"]):
             E("t", s - OFF["Et"])
             Bq(s - OFF["B"])
             M2("s", s - OFF["I"])
-            C("t", s - OFF["Ct"], "v" if s - OFF["Ct"] < CT_ON_V else "s")
-            C("s", s - OFF["Cs"], "s")
+            for n in chunks(s, OFF["Ct"]):
+                C("t", n, "v" if n < CT_ON_V else "s")
+            for n in chunks(s, OFF["Cs"]):
+                C("s", n, "s")
             A(s, "v" if s < A_ON_V else "s")
-            M1("t", s + 1 - OFF["Ct"])
-            T(s + 1)
-            M1("s", s + 1 - OFF["Cs"])
+            for n in chunks(s + 1, OFF["Ct"]):
+                M1("t", n)
+            for n in chunks(s + 1, OFF["Cs"]):
+                M1("s", n)
+            if s % 2 == 1:
+                T(s + 1)
+                T(s + 2)
             D("t", s - OFF["Dt"], "s" if s - OFF["Dt"] >= DT_ON_S_FROM else "v")
             D("s", s - OFF["Ds"], "s")
             X(s - OFF["X"])
@@ -361,5 +365,5 @@ def tile_madesplit_pa_t_kernel(
             if s % 4 == 0:
                 LD("t", s // 4 + 3)
                 LD("s", s // 4 + 3)
-                LD("x", s // 4 + 2)
+                LD("x", s // 4 + 1)
         nc.sync.dma_start(out=out_1.rearrange("(p i) o -> p (i o)", i=ROWS), in_=ld[:])

@@ -23,6 +23,8 @@ FLOPS = 4 * 2 * B * H * N
 PINNED = True
 H_PIECE = 256
 XB_BUFS = 6
+HALF = {"t": 0, "s": 1}
+DS_ON_V = (3,)
 OFF = {"B": 1, "Ct": 3, "Cs": 5, "Dt": 5, "Et": 6, "F": 7, "X": 8, "Ds": 6, "Es": 7, "I": 8, "J": 9, "H": 3}
 A_ON_V = 0
 CT_ON_V = 6
@@ -186,36 +188,35 @@ def tile_madesplit_pa_t_kernel(
             if not ok(n):
                 return
             g, q = divmod(n, 4)
-            if q == 0:
-                st[("g2", nm, g)] = two.tile([P, 512, 4], BF16, name="g2_" + nm, tag="g2_" + nm, align_bytes=64)
+            key = ("g2", n + OFF["E" + nm])
+            if key not in st:
+                st[key] = three.tile([P, 2, 128, 4], BF16, name="g2", tag="g2", align_bytes=64)
             c = slice(128 * q, 128 * q + 128)
             copy_on(
                 eng,
-                st[("g2", nm, g)][:, c, :].rearrange("p (c i) t -> p c t i", i=4),
+                st[key][:, HALF[nm], :, :].rearrange("p (c i) t -> p c t i", i=4),
                 st[("hT", nm, g)][:, :, c].rearrange("p t (c i) -> p c t i", i=4),
             )
 
-        def E(nm, n):
-            if not ok(n):
+        def E(s):
+            c0 = 0 if ok(s - OFF["Et"]) else 128
+            c1 = 256 if ok(s - OFF["Es"]) else 128
+            if c0 == c1:
                 return
-            g, q = divmod(n, 4)
-            if q == 0:
-                st[("c2", nm, g)] = two.tile([P, 512], U32, name="c2_" + nm, tag="c2_" + nm, align_bytes=64)
-                st[("s2", nm, g)] = two.tile([P, 512], U8, name="s2_" + nm, tag="s2_" + nm, align_bytes=64)
-            quantise(
-                st[("g2", nm, g)][:].rearrange("p c t -> p (c t)"), st[("c2", nm, g)], st[("s2", nm, g)],
-                128 * q, 128 * q + 128,
-            )
+            st[("c2", s)] = three.tile([P, 256], U32, name="c2", tag="c2", align_bytes=64)
+            st[("s2", s)] = three.tile([P, 256], U8, name="s2", tag="s2", align_bytes=64)
+            quantise(st[("g2", s)][:].rearrange("p h c t -> p (h c t)"), st[("c2", s)], st[("s2", s)], c0, c1)
 
         def M2(nm, n):
             if not ok(n):
                 return
-            g, q = divmod(n, 4)
+            key = n + OFF["E" + nm]
+            h = HALF[nm]
             acc = ps1.tile([P, 512], F32, name="m2" + nm, tag="m2" + nm)
             nc.tensor.matmul_mx(
                 out=acc[:],
-                lhsT=st[("c2", nm, g)][:, 128 * q : 128 * q + 128].bitcast(FP8X4),
-                lhsT_scale=st[("s2", nm, g)][:, 128 * q : 128 * q + 128],
+                lhsT=st[("c2", key)][:, 128 * h : 128 * h + 128].bitcast(FP8X4),
+                lhsT_scale=st[("s2", key)][:, 128 * h : 128 * h + 128],
                 rhs=st[("wc", nm + "3")][:].bitcast(FP8X4),
                 rhs_scale=st[("ws", nm + "3")][:],
                 start=True,
@@ -338,7 +339,6 @@ def tile_madesplit_pa_t_kernel(
         T(0)
         T(1)
         for s in range(ITEMS + OFF["J"]):
-            E("t", s - OFF["Et"])
             Bq(s - OFF["B"])
             M2("s", s - OFF["I"])
             for n in chunks(s, OFF["Ct"]):
@@ -354,10 +354,10 @@ def tile_madesplit_pa_t_kernel(
                 T(s + 1)
                 T(s + 2)
             D("t", s - OFF["Dt"], "s" if s - OFF["Dt"] >= DT_ON_S_FROM else "v")
-            D("s", s - OFF["Ds"], "s")
+            D("s", s - OFF["Ds"], "v" if (s - OFF["Ds"]) % 4 in DS_ON_V and s - OFF["Ds"] < DT_ON_S_FROM else "s")
             X(s - OFF["X"])
             J(s - OFF["J"])
-            E("s", s - OFF["Es"])
+            E(s)
             Fa(s - OFF["F"])
             M2("t", s + 1 - OFF["F"])
             Im(s - OFF["I"])

@@ -26,11 +26,12 @@ XB_BUFS = 6
 HALF = {"t": 0, "s": 1}
 DS_ON_V = (3,)
 OFF = {"B": 1, "Ct": 3, "Cs": 5, "Dt": 5, "Et": 6, "F": 7, "X": 8, "Ds": 6, "Es": 7, "I": 8, "J": 9, "H": 3}
+LAST_C_STEP = ITEMS - 4 + OFF["Cs"] + 1
 A_ON_V = 0
 CT_ON_V = 6
 DT_ON_S_FROM = 24
 MASK_ON_G = ()
-J_ON_G = (26, 27, 28, 29, 30)
+J_ON_G = (26, 27, 28, 29)
 
 
 def tile_madesplit_pa_t_kernel(
@@ -212,7 +213,10 @@ def tile_madesplit_pa_t_kernel(
                 return
             key = n + OFF["E" + nm]
             h = HALF[nm]
-            acc = ps1.tile([P, 512], F32, name="m2" + nm, tag="m2" + nm)
+            if key + HALF[nm] > LAST_C_STEP:
+                acc = ps2.tile([P, 512], F32, name="m1", tag="m1", bufs=4)
+            else:
+                acc = ps1.tile([P, 512], F32, name="m2" + nm, tag="m2" + nm)
             nc.tensor.matmul_mx(
                 out=acc[:],
                 lhsT=st[("c2", key)][:, 128 * h : 128 * h + 128].bitcast(FP8X4),

from contextlib import ExitStack

import concourse.mybir as mybir
from concourse.masks import make_identity

F32 = mybir.dt.float32
BF16 = mybir.dt.bfloat16
U32 = mybir.dt.uint32
U8 = mybir.dt.uint8
FP8X4 = mybir.dt.float8_e4m3fn_x4
ACT = mybir.ActivationFunctionType
ALU = mybir.AluOpType

P = 128
B, N, H = 4096, 512, 512
G = 8
R = 4
ROWS = B // P
ITEMS = G * R

FLOPS = 4 * 2 * B * H * N

PINNED = True
H_PIECE = 256
XB_BUFS = 6
HALF = {"t": 0, "s": 1}
DS_ON_V = (3,)
OFF = {"B": 1, "Ct": 3, "Cs": 5, "Dt": 5, "Et": 6, "F": 7, "X": 8, "Ds": 6, "Es": 7, "I": 8, "J": 9, "H": 3}
LAST_C_STEP = ITEMS - 4 + OFF["Cs"] + 1
A_ON_V = 0
CT_ON_V = 6
DT_ON_S_FROM = 24
MASK_ON_G = ()
J_ON_G = (26, 27, 28, 29)


def tile_madesplit_pa_t_kernel(
    tc, inputs, h_s1, h_t1, s_w2, s_b2, s_w3, s_b3, t_w2, t_b2, t_w3, t_b3, mask_hid, mask_out, out_0, out_1
):
    nc = tc.nc
    with ExitStack() as ctx:
        const = ctx.enter_context(tc.tile_pool(name="const", bufs=1))
        wgrp_pool = ctx.enter_context(tc.tile_pool(name="wgrp", bufs=2))
        raw_pool = ctx.enter_context(tc.tile_pool(name="raw", bufs=3))
        two = ctx.enter_context(tc.tile_pool(name="two", bufs=2))
        three = ctx.enter_context(tc.tile_pool(name="three", bufs=3))
        ps2 = ctx.enter_context(tc.psum_pool(name="ps2", bufs=2))
        ps1 = ctx.enter_context(tc.psum_pool(name="ps1", bufs=1))

        views = {
            "x": inputs.rearrange("(p i) n -> p i n", i=ROWS),
            "s": h_s1.rearrange("(p i) k -> p i k", i=ROWS),
            "t": h_t1.rearrange("(p i) k -> p i k", i=ROWS),
        }
        u_v = out_0.rearrange("(p i) n -> p i n", i=ROWS)

        ident = const.tile([P, P], F32, name="ident")
        make_identity(nc, ident[:])
        ones = const.tile([P, P], BF16, name="ones")
        nc.vector.memset(ones[:], 1.0)

        st = {}

        def ok(n):
            return 0 <= n < ITEMS

        def copy_on(eng, out, in_):
            if eng == "v":
                nc.vector.tensor_copy(out=out, in_=in_)
            else:
                nc.scalar.copy(out=out, in_=in_)

        def LD(nm, g):
            if not 0 <= g < G:
                return
            t = raw_pool.tile([P, R * 512], BF16, name="raw_" + nm, tag="raw_" + nm, bufs=4 if nm == "x" else 3)
            nc.sync.dma_start(out=t[:].rearrange("p (r k) -> p r k", r=R), in_=views[nm][:, R * g : R * g + R, :])
            st[("raw", nm, g)] = t

        w_dram = {"s2": s_w2, "t2": t_w2, "mh": mask_hid, "s3": s_w3, "t3": t_w3, "mo": mask_out}

        def LDW(nm, h):
            if h == 0:
                st[("w", nm)] = const.tile([P, 2048], BF16, name="w_" + nm)
            t = st[("w", nm)]
            if nm in ("s2", "t2", "mh"):
                src = w_dram[nm].rearrange("(u p e) k -> u p e k", u=2, e=2)[h]
                nc.sync.dma_start(out=t[:, 1024 * h : 1024 * h + 1024].rearrange("p (e k) -> p e k", e=2), in_=src)
            else:
                src = w_dram[nm].rearrange("(r p) k -> p r k", p=P)[:, 2 * h : 2 * h + 2, :]
                nc.sync.dma_start(out=t[:, 1024 * h : 1024 * h + 1024].rearrange("p (r k) -> p r k", r=2), in_=src)

        def turn(src, h, tag, pool):
            bank = pool.tile([P, 2, 256], F32, name="bank_" + tag, tag=tag)
            srcw = src[:].bitcast(F32)
            for rr in range(2):
                for u in range(2):
                    o = 256 * (2 * h + rr) + 128 * u
                    nc.tensor.transpose(bank[:, u, 128 * rr : 128 * rr + 128], srcw[:, o : o + 128], ident[:])
            return bank

        def out_of_bank(bank, grouped, h, eng):
            dstw = grouped[:].bitcast(F32).rearrange("p (c u) -> p c u", u=2)
            copy_on(eng, dstw[:, 256 * h : 256 * h + 256, :], bank[:].rearrange("p u c -> p c u"))

        def quantise(grouped2d, codes, scales, c0, c1):
            nc.vector.quantize_mx(
                out=codes[:, c0:c1].bitcast(FP8X4), scales=scales[:, c0:c1], in_=grouped2d[:, 4 * c0 : 4 * c1]
            )

        def prep_w(nm, mask, h, eng, tag, pool):
            t = st[("w", nm)]
            sl = slice(1024 * h, 1024 * h + 1024)
            if nm in MASK_ON_G:
                for c in range(1024 * h, 1024 * h + 1024, H_PIECE):
                    nc.gpsimd.tensor_tensor(
                        out=t[:, c : c + H_PIECE], in0=t[:, c : c + H_PIECE], in1=st[("w", mask)][:, c : c + H_PIECE],
                        op=ALU.mult,
                    )
            else:
                nc.vector.tensor_tensor(out=t[:, sl], in0=t[:, sl], in1=st[("w", mask)][:, sl], op=ALU.mult)
            if h == 0:
                st[("wg", nm)] = wgrp_pool.tile([P, 2048], BF16, name="wgrp", tag="wgrp", align_bytes=64)
                st[("wc", nm)] = const.tile([P, 512], U32, name="wc_" + nm, align_bytes=64)
                st[("ws", nm)] = const.tile([P, 512], U8, name="ws_" + nm, align_bytes=64)
            bank = turn(t, h, tag, pool)
            out_of_bank(bank, st[("wg", nm)], h, eng)
            quantise(st[("wg", nm)], st[("wc", nm)], st[("ws", nm)], 256 * h, 256 * h + 256)

        def T(n):
            if not ok(n):
                return
            g, q = divmod(n, 4)
            nm = "t" if q < 2 else "s"
            st[("b0", n)] = turn(st[("raw", nm, g)], q % 2, "tp", ps2)

        def A(n, eng):
            if not ok(n):
                return
            g, q = divmod(n, 4)
            nm = "t" if q < 2 else "s"
            if q % 2 == 0:
                st[("g1", nm, g)] = two.tile([P, 2048], BF16, name="g1_" + nm, tag="g1_" + nm, align_bytes=64)
            out_of_bank(st[("b0", n)], st[("g1", nm, g)], q % 2, eng)

        def Bq(n):
            if not ok(n):
                return
            g, q = divmod(n, 4)
            nm = "t" if q < 2 else "s"
            h = q % 2
            if h == 0:
                st[("c1", nm, g)] = three.tile([P, 512], U32, name="c1_" + nm, tag="c1_" + nm, align_bytes=64)
                st[("s1", nm, g)] = three.tile([P, 512], U8, name="s1_" + nm, tag="s1_" + nm, align_bytes=64)
            quantise(st[("g1", nm, g)], st[("c1", nm, g)], st[("s1", nm, g)], 256 * h, 256 * h + 256)

        def M1(nm, n):
            if not ok(n):
                return
            g, j = divmod(n, 4)
            acc = ps2.tile([P, 512], F32, name="m1", tag="m1", bufs=4)
            nc.tensor.matmul_mx(
                out=acc[:],
                lhsT=st[("wc", nm + "2")][:, 128 * j : 128 * j + 128].bitcast(FP8X4),
                lhsT_scale=st[("ws", nm + "2")][:, 128 * j : 128 * j + 128],
                rhs=st[("c1", nm, g)][:].bitcast(FP8X4),
                rhs_scale=st[("s1", nm, g)][:],
                start=True,
                stop=True,
            )
            st[("a1", nm, n)] = acc

        def C(nm, n, eng):
            if not ok(n):
                return
            g, j = divmod(n, 4)
            if j == 0:
                st[("hT", nm, g)] = two.tile([P, 4, 512], BF16, name="hT_" + nm, tag="hT_" + nm)
            dst = st[("hT", nm, g)][:, j, :]
            acc = st[("a1", nm, n)]
            boff = 0 if nm == "s" else 4
            bias = b2f[:, boff + j : boff + j + 1]
            if eng == "v":
                nc.vector.tensor_scalar(out=dst, in0=acc[:], scalar1=bias, scalar2=0.0, op0=ALU.add, op1=ALU.max)
            else:
                nc.scalar.activation(out=dst, in_=acc[:], func=ACT.Tanh if nm == "s" else ACT.Relu, bias=bias, scale=1.0)

        def D(nm, n, eng):
            if not ok(n):
                return
            g, q = divmod(n, 4)
            key = ("g2", n + OFF["E" + nm])
            if key not in st:
                st[key] = three.tile([P, 2, 128, 4], BF16, name="g2", tag="g2", align_bytes=64)
            c = slice(128 * q, 128 * q + 128)
            copy_on(
                eng,
                st[key][:, HALF[nm], :, :].rearrange("p (c i) t -> p c t i", i=4),
                st[("hT", nm, g)][:, :, c].rearrange("p t (c i) -> p c t i", i=4),
            )

        def E(s):
            c0 = 0 if ok(s - OFF["Et"]) else 128
            c1 = 256 if ok(s - OFF["Es"]) else 128
            if c0 == c1:
                return
            st[("c2", s)] = three.tile([P, 256], U32, name="c2", tag="c2", align_bytes=64)
            st[("s2", s)] = three.tile([P, 256], U8, name="s2", tag="s2", align_bytes=64)
            quantise(st[("g2", s)][:].rearrange("p h c t -> p (h c t)"), st[("c2", s)], st[("s2", s)], c0, c1)

        def M2(nm, n):
            if not ok(n):
                return
            key = n + OFF["E" + nm]
            h = HALF[nm]
            if key + HALF[nm] > LAST_C_STEP:
                acc = ps2.tile([P, 512], F32, name="m1", tag="m1", bufs=4)
            else:
                acc = ps1.tile([P, 512], F32, name="m2" + nm, tag="m2" + nm)
            nc.tensor.matmul_mx(
                out=acc[:],
                lhsT=st[("c2", key)][:, 128 * h : 128 * h + 128].bitcast(FP8X4),
                lhsT_scale=st[("s2", key)][:, 128 * h : 128 * h + 128],
                rhs=st[("wc", nm + "3")][:].bitcast(FP8X4),
                rhs_scale=st[("ws", nm + "3")][:],
                start=True,
                stop=True,
            )
            st[("a2", nm, n)] = acc

        def Hx(n):
            if not ok(n):
                return
            g, q = divmod(n, 4)
            st[("xb", n)] = two.tile([P, 512], F32, name="xb", tag="xb", bufs=XB_BUFS)
            xr = st[("raw", "x", g)]
            nc.gpsimd.tensor_tensor(
                out=st[("xb", n)][:], in0=xr[:, 512 * q : 512 * q + 512], in1=nb3s[:], op=ALU.add
            )

        def Fa(n):
            if not ok(n):
                return
            g, q = divmod(n, 4)
            if q == 0:
                st[("na", g)] = three.tile([P, R, 512], F32, name="na", tag="na")
            nc.vector.scalar_tensor_tensor(
                out=st[("na", g)][:, q, :], in0=st[("a2", "t", n)][:], scalar=-1.0, in1=nb3t[:],
                op0=ALU.mult, op1=ALU.add, accum_out=ld[:, n : n + 1],
            )

        def Im(n):
            if not ok(n):
                return
            nc.vector.scalar_tensor_tensor(
                out=st[("xb", n)][:], in0=st[("a2", "s", n)][:], scalar=-1.0, in1=st[("xb", n)][:],
                op0=ALU.mult, op1=ALU.add,
            )

        def X(n):
            if not ok(n):
                return
            g, q = divmod(n, 4)
            nc.scalar.activation(out=st[("na", g)][:, q, :], in_=st[("na", g)][:, q, :], func=ACT.Exp)

        def J(n):
            if not ok(n):
                return
            g, q = divmod(n, 4)
            d = st[("xb", n)]
            u = st[("na", g)]
            if n in J_ON_G:
                for c in range(0, 512, H_PIECE):
                    nc.gpsimd.tensor_tensor(
                        out=u[:, q, c : c + H_PIECE], in0=d[:, c : c + H_PIECE],
                        in1=u[:, q, c : c + H_PIECE], op=ALU.mult,
                    )
            else:
                nc.vector.tensor_tensor(out=u[:, q, :], in0=d[:], in1=u[:, q, :], op=ALU.mult)
            if g == G - 1:
                nc.sync.dma_start(out=u_v[:, n, :], in_=u[:, q, :])
            elif q == R - 1:
                nc.sync.dma_start(out=u_v[:, R * g : R * g + R, :], in_=u[:])

        LDW("t2", 0)
        LDW("mh", 0)
        LD("t", 0)
        LDW("t2", 1)
        LDW("mh", 1)
        b2rows = const.tile([P, 256], BF16, name="b2rows")
        nc.vector.memset(b2rows[:], 0.0)
        nc.sync.dma_start(out=b2rows[0:2, :], in_=s_b2.rearrange("(u c) -> u c", u=2))
        nc.sync.dma_start(out=b2rows[2:4, :], in_=t_b2.rearrange("(u c) -> u c", u=2))
        LD("s", 0)
        LDW("s2", 0)
        LDW("s2", 1)
        LD("t", 1)
        LD("s", 1)
        b3rows = const.tile([P, 1024], BF16, name="b3rows")
        nc.vector.memset(b3rows[:], 0.0)
        nc.sync.dma_start(out=b3rows[0:1, 0:512], in_=s_b3.rearrange("(o c) -> o c", o=1))
        nc.sync.dma_start(out=b3rows[0:1, 512:1024], in_=t_b3.rearrange("(o c) -> o c", o=1))
        for nm in ("t3", "mo", "s3"):
            LDW(nm, 0)
            LDW(nm, 1)
        LD("x", 0)
        LD("t", 2)
        LD("s", 2)

        prep_w("t2", "mh", 0, "s", "m2t", ps1)
        prep_w("t2", "mh", 1, "s", "m2s", ps1)

        bank_b = ps1.tile([P, P], F32, name="bank_b", tag="m2t")
        nc.tensor.transpose(bank_b[:], b2rows[:].bitcast(F32), ident[:])
        b2w = const.tile([P, 4], F32, name="b2w")
        nc.vector.tensor_copy(out=b2w[:], in_=bank_b[:, 0:4])
        b2f = const.tile([P, 8], F32, name="b2f")
        nc.vector.tensor_copy(out=b2f[:], in_=b2w[:].bitcast(BF16))

        prep_w("s2", "mh", 0, "s", "m2t", ps1)
        prep_w("s2", "mh", 1, "s", "m2s", ps1)

        nb3s = const.tile([P, 512], F32, name="nb3s")
        nb3t = const.tile([P, 512], F32, name="nb3t")
        for dst, off, tag in ((nb3s, 0, "m2t"), (nb3t, 512, "m2s")):
            bank_c = ps1.tile([P, 512], F32, name="bank_c", tag=tag)
            nc.tensor.matmul(out=bank_c[:], lhsT=ones[:], rhs=b3rows[:, off : off + 512], start=True, stop=True)
            nc.scalar.mul(out=dst[:], in_=bank_c[:], mul=-1.0)
        ld = const.tile([P, ROWS], F32, name="ld")

        prep_w("t3", "mo", 0, "s", "m2t", ps1)
        prep_w("t3", "mo", 1, "s", "m2s", ps1)
        prep_w("s3", "mo", 0, "s", "m2t", ps1)
        prep_w("s3", "mo", 1, "s", "m2s", ps1)

        if PINNED:
            ctx.enter_context(tc.manual_schedule())

        def chunks(s, off):
            g, r = divmod(s - off, 4)
            return (4 * g + 2 * r, 4 * g + 2 * r + 1) if r < 2 else ()

        T(0)
        T(1)
        for s in range(ITEMS + OFF["J"]):
            Bq(s - OFF["B"])
            M2("s", s - OFF["I"])
            for n in chunks(s, OFF["Ct"]):
                C("t", n, "v" if n < CT_ON_V else "s")
            for n in chunks(s, OFF["Cs"]):
                C("s", n, "s")
            A(s, "v" if s < A_ON_V else "s")
            for n in chunks(s + 1, OFF["Ct"]):
                M1("t", n)
            for n in chunks(s + 1, OFF["Cs"]):
                M1("s", n)
            if s % 2 == 1:
                T(s + 1)
                T(s + 2)
            D("t", s - OFF["Dt"], "s" if s - OFF["Dt"] >= DT_ON_S_FROM else "v")
            D("s", s - OFF["Ds"], "v" if (s - OFF["Ds"]) % 4 in DS_ON_V and s - OFF["Ds"] < DT_ON_S_FROM else "s")
            X(s - OFF["X"])
            J(s - OFF["J"])
            E(s)
            Fa(s - OFF["F"])
            M2("t", s + 1 - OFF["F"])
            Im(s - OFF["I"])
            Hx(s - OFF["H"])
            if s % 4 == 0:
                LD("t", s // 4 + 3)
                LD("s", s // 4 + 3)
                LD("x", s // 4 + 1)
        nc.sync.dma_start(out=out_1.rearrange("(p i) o -> p (i o)", i=ROWS), in_=ld[:])
